import numpy as np
import ml_dtypes

BF16 = ml_dtypes.bfloat16


def bf(x):
    return np.asarray(x, np.float32).astype(BF16)


def f32(x):
    return np.asarray(x, np.float32)


def f64(x):
    return np.asarray(x).astype(np.float64)


def striped(idx):
    return np.tile(idx.reshape(-1, 16).T, (8, 1))


S, D, M, N, W = 4096, 128, 256, 512, 8


def setup_inputs():
    return {"table": bf(np.random.standard_normal((S, D))), "w": bf(np.random.standard_normal((D, M)) / np.sqrt(D)), "offs": striped(np.random.permutation(S)[:N])}


def reference(table, w, offs):
    idx = offs[:16].T.reshape(-1)
    mm = f64(w).T @ f64(table)[idx].T
    return mm.reshape(M, W, N // W).sum(axis=1)

@@ -1,0 +1,67 @@
+import concourse.mybir as mybir
+from concourse.masks import make_identity
+
+BF16, F32, U16 = mybir.dt.bfloat16, mybir.dt.float32, mybir.dt.uint16
+
+P = 128
+STORE = 4096
+FEATURES_OUT = 256
+PICKED = 512
+CHUNKS = 8
+CHUNK = PICKED // CHUNKS
+BLOCKS = STORE // P
+BLOCKS_IN_BANK = 8
+GROUPS = BLOCKS // BLOCKS_IN_BANK
+GROUP_TOKENS = BLOCKS_IN_BANK * P
+
+FLOPS = 2 * P * FEATURES_OUT * PICKED
+
+
+def tile_testmmrsmodel_kernel(tc, table, w, offs, out):
+    nc = tc.nc
+    with (
+        tc.tile_pool(name="held", bufs=1) as held,
+        tc.tile_pool(name="sums", bufs=2) as sums,
+        tc.psum_pool(name="flipped", bufs=2) as flipped,
+        tc.psum_pool(name="products", bufs=2) as products,
+    ):
+        offsets = held.tile([P, PICKED // 16], U16, name="offsets")
+        nc.sync.dma_start(offsets[:], offs)
+
+        rows = held.tile([P, BLOCKS, P], BF16, name="rows")
+        table_blocks = table.rearrange("(b p) d -> p b d", p=P)
+        for g in range(GROUPS):
+            blocks = slice(g * BLOCKS_IN_BANK, (g + 1) * BLOCKS_IN_BANK)
+            queue = nc.sync if g % 2 == 0 else nc.scalar
+            queue.dma_start(rows[:, blocks, :], table_blocks[:, blocks, :])
+
+        weights = held.tile([P, FEATURES_OUT], BF16, name="weights")
+        nc.gpsimd.dma_start(weights[:], w)
+
+        identity = held.tile([P, P], BF16, name="identity")
+        make_identity(nc, identity[:])
+
+        window = held.tile([P, STORE], BF16, name="window")
+        for g in range(GROUPS):
+            bank = flipped.tile([P, GROUP_TOKENS], BF16, name="bank")
+            for j in range(BLOCKS_IN_BANK):
+                nc.tensor.transpose(bank[:, j * P : (j + 1) * P], rows[:, g * BLOCKS_IN_BANK + j, :], identity[:])
+            tokens = slice(g * GROUP_TOKENS, (g + 1) * GROUP_TOKENS)
+            if g % 2 == 0:
+                nc.vector.tensor_copy(window[:, tokens], bank[:])
+            else:
+                nc.scalar.copy(window[:, tokens], bank[:])
+
+        for h in range(FEATURES_OUT // P):
+            product = products.tile([P, PICKED], F32, name="product")
+            nc.tensor.matmul(
+                product[:], weights[:, h * P : (h + 1) * P], window[:].indirect(offsets[:]), start=True, stop=True
+            )
+            summed = sums.tile([P, CHUNK], F32, name="summed")
+            nc.vector.tensor_reduce(
+                summed[:],
+                product[:].rearrange("p (c r) -> p r c", c=CHUNKS),
+                axis=mybir.AxisListType.X,
+                op=mybir.AluOpType.add,
+            )
+            nc.sync.dma_start(out[h * P : (h + 1) * P, :], summed[:])

@@ -9,10 +9,9 @@ FEATURES_OUT = 256
 PICKED = 512
 CHUNKS = 8
 CHUNK = PICKED // CHUNKS
-BLOCKS = STORE // P
-BLOCKS_IN_BANK = 8
-GROUPS = BLOCKS // BLOCKS_IN_BANK
-GROUP_TOKENS = BLOCKS_IN_BANK * P
+LOADS = 8
+BLOCKS_IN_LOAD = STORE // P // LOADS
+PAIR = 2 * P
 
 FLOPS = 2 * P * FEATURES_OUT * PICKED
 
@@ -21,36 +20,33 @@ def tile_testmmrsmodel_kernel(tc, table, w, offs, out):
     nc = tc.nc
     with (
         tc.tile_pool(name="held", bufs=1) as held,
+        tc.tile_pool(name="rows", bufs=LOADS) as rows,
         tc.tile_pool(name="sums", bufs=2) as sums,
-        tc.psum_pool(name="flipped", bufs=2) as flipped,
+        tc.psum_pool(name="flipped", bufs=6) as flipped,
         tc.psum_pool(name="products", bufs=2) as products,
     ):
-        offsets = held.tile([P, PICKED // 16], U16, name="offsets")
-        nc.sync.dma_start(offsets[:], offs)
-
-        rows = held.tile([P, BLOCKS, P], BF16, name="rows")
-        table_blocks = table.rearrange("(b p) d -> p b d", p=P)
-        for g in range(GROUPS):
-            blocks = slice(g * BLOCKS_IN_BANK, (g + 1) * BLOCKS_IN_BANK)
-            queue = nc.sync if g % 2 == 0 else nc.scalar
-            queue.dma_start(rows[:, blocks, :], table_blocks[:, blocks, :])
-
-        weights = held.tile([P, FEATURES_OUT], BF16, name="weights")
-        nc.gpsimd.dma_start(weights[:], w)
-
         identity = held.tile([P, P], BF16, name="identity")
         make_identity(nc, identity[:])
 
         window = held.tile([P, STORE], BF16, name="window")
-        for g in range(GROUPS):
-            bank = flipped.tile([P, GROUP_TOKENS], BF16, name="bank")
-            for j in range(BLOCKS_IN_BANK):
-                nc.tensor.transpose(bank[:, j * P : (j + 1) * P], rows[:, g * BLOCKS_IN_BANK + j, :], identity[:])
-            tokens = slice(g * GROUP_TOKENS, (g + 1) * GROUP_TOKENS)
-            if g % 2 == 0:
-                nc.vector.tensor_copy(window[:, tokens], bank[:])
-            else:
-                nc.scalar.copy(window[:, tokens], bank[:])
+        table_blocks = table.rearrange("(b p) d -> p b d", p=P)
+        for l in range(LOADS):
+            loaded = rows.tile([P, BLOCKS_IN_LOAD, P], BF16, name="loaded")
+            nc.sync.dma_start(loaded[:], table_blocks[:, l * BLOCKS_IN_LOAD : (l + 1) * BLOCKS_IN_LOAD, :])
+            for k in range(BLOCKS_IN_LOAD // 2):
+                pair = flipped.tile([P, PAIR], BF16, name="pair")
+                for j in range(2):
+                    nc.tensor.transpose(pair[:, j * P : (j + 1) * P], loaded[:, 2 * k + j, :], identity[:])
+                first = (l * BLOCKS_IN_LOAD + 2 * k) * P
+                if k % 2 == 0:
+                    nc.vector.tensor_copy(window[:, first : first + PAIR], pair[:])
+                else:
+                    nc.scalar.copy(window[:, first : first + PAIR], pair[:])
+
+        offsets = held.tile([P, PICKED // 16], U16, name="offsets")
+        nc.sync.dma_start(offsets[:], offs)
+        weights = held.tile([P, FEATURES_OUT], BF16, name="weights")
+        nc.gpsimd.dma_start(weights[:], w)
 
         for h in range(FEATURES_OUT // P):
             product = products.tile([P, PICKED], F32, name="product")
@@ -64,4 +60,5 @@ def tile_testmmrsmodel_kernel(tc, table, w, offs, out):
                 axis=mybir.AxisListType.X,
                 op=mybir.AluOpType.add,
             )
-            nc.sync.dma_start(out[h * P : (h + 1) * P, :], summed[:])
+            queue = nc.sync if h == 0 else nc.scalar
+            queue.dma_start(out[h * P : (h + 1) * P, :], summed[:])

@@ -12,6 +12,7 @@ CHUNK = PICKED // CHUNKS
 LOADS = 8
 BLOCKS_IN_LOAD = STORE // P // LOADS
 PAIR = 2 * P
+WARM_UP = 5
 
 FLOPS = 2 * P * FEATURES_OUT * PICKED
 
@@ -22,9 +23,16 @@ def tile_testmmrsmodel_kernel(tc, table, w, offs, out):
         tc.tile_pool(name="held", bufs=1) as held,
         tc.tile_pool(name="rows", bufs=LOADS) as rows,
         tc.tile_pool(name="sums", bufs=2) as sums,
-        tc.psum_pool(name="flipped", bufs=6) as flipped,
+        tc.psum_pool(name="flipped", bufs=5) as flipped,
         tc.psum_pool(name="products", bufs=2) as products,
+        tc.psum_pool(name="unused", bufs=1) as unused,
     ):
+        zeros = held.tile([P, PICKED], BF16, name="zeros")
+        nc.vector.memset(zeros[:], 0.0)
+        nothing = unused.tile([P, PICKED], F32, name="nothing")
+        for turn in range(WARM_UP):
+            nc.tensor.matmul(nothing[:], zeros[:, :P], zeros[:], start=True, stop=True)
+
         identity = held.tile([P, P], BF16, name="identity")
         make_identity(nc, identity[:])
 

@@ -50,6 +50,7 @@ def tile_testmmrsmodel_kernel(tc, table, w, offs, out):
                     nc.vector.tensor_copy(window[:, first : first + PAIR], pair[:])
                 else:
                     nc.scalar.copy(window[:, first : first + PAIR], pair[:])
+            nc.tensor.matmul(nothing[:], identity[:], loaded[:].rearrange("p b d -> p (b d)"), start=True, stop=True)
 
         offsets = held.tile([P, PICKED // 16], U16, name="offsets")
         nc.sync.dma_start(offsets[:], offs)

@@ -10,9 +10,10 @@ PICKED = 512
 CHUNKS = 8
 CHUNK = PICKED // CHUNKS
 LOADS = 8
-BLOCKS_IN_LOAD = STORE // P // LOADS
-PAIR = 2 * P
+GROUP = 2 * P
+GROUPS_IN_LOAD = STORE // GROUP // LOADS
 WARM_UP = 5
+IDLE_COLUMNS = 384
 
 FLOPS = 2 * P * FEATURES_OUT * PICKED
 
@@ -37,20 +38,27 @@ def tile_testmmrsmodel_kernel(tc, table, w, offs, out):
         make_identity(nc, identity[:])
 
         window = held.tile([P, STORE], BF16, name="window")
-        table_blocks = table.rearrange("(b p) d -> p b d", p=P)
+        table_groups = table.rearrange("(g p j) d -> p g j d", p=P, j=2)
         for l in range(LOADS):
-            loaded = rows.tile([P, BLOCKS_IN_LOAD, P], BF16, name="loaded")
-            nc.sync.dma_start(loaded[:], table_blocks[:, l * BLOCKS_IN_LOAD : (l + 1) * BLOCKS_IN_LOAD, :])
-            for k in range(BLOCKS_IN_LOAD // 2):
-                pair = flipped.tile([P, PAIR], BF16, name="pair")
+            loaded = rows.tile([P, GROUPS_IN_LOAD, 2, P], BF16, name="loaded")
+            nc.sync.dma_start(loaded[:], table_groups[:, l * GROUPS_IN_LOAD : (l + 1) * GROUPS_IN_LOAD, :, :])
+            for k in range(GROUPS_IN_LOAD):
+                flipped_group = flipped.tile([P, 2, P], BF16, name="flipped_group")
                 for j in range(2):
-                    nc.tensor.transpose(pair[:, j * P : (j + 1) * P], loaded[:, 2 * k + j, :], identity[:])
-                first = (l * BLOCKS_IN_LOAD + 2 * k) * P
+                    nc.tensor.transpose(flipped_group[:, j, :], loaded[:, k, j, :], identity[:])
+                first = (l * GROUPS_IN_LOAD + k) * GROUP
+                columns = window[:, first : first + GROUP].rearrange("d (p j) -> d p j", j=2)
                 if k % 2 == 0:
-                    nc.vector.tensor_copy(window[:, first : first + PAIR], pair[:])
+                    nc.vector.tensor_copy(columns, flipped_group[:].rearrange("d j p -> d p j"))
                 else:
-                    nc.scalar.copy(window[:, first : first + PAIR], pair[:])
-            nc.tensor.matmul(nothing[:], identity[:], loaded[:].rearrange("p b d -> p (b d)"), start=True, stop=True)
+                    nc.scalar.copy(columns, flipped_group[:].rearrange("d j p -> d p j"))
+            nc.tensor.matmul(
+                nothing[:, :IDLE_COLUMNS],
+                identity[:],
+                loaded[:].rearrange("p k j d -> p (k j d)")[:, :IDLE_COLUMNS],
+                start=True,
+                stop=True,
+            )
 
         offsets = held.tile([P, PICKED // 16], U16, name="offsets")
         nc.sync.dma_start(offsets[:], offs)

@@ -9,11 +9,9 @@ FEATURES_OUT = 256
 PICKED = 512
 CHUNKS = 8
 CHUNK = PICKED // CHUNKS
-LOADS = 8
 GROUP = 2 * P
-GROUPS_IN_LOAD = STORE // GROUP // LOADS
-WARM_UP = 5
-IDLE_COLUMNS = 384
+LOADS = STORE // GROUP
+WARM_UP = 4
 
 FLOPS = 2 * P * FEATURES_OUT * PICKED
 
@@ -38,26 +36,20 @@ def tile_testmmrsmodel_kernel(tc, table, w, offs, out):
         make_identity(nc, identity[:])
 
         window = held.tile([P, STORE], BF16, name="window")
-        table_groups = table.rearrange("(g p j) d -> p g j d", p=P, j=2)
-        for l in range(LOADS):
-            loaded = rows.tile([P, GROUPS_IN_LOAD, 2, P], BF16, name="loaded")
-            nc.sync.dma_start(loaded[:], table_groups[:, l * GROUPS_IN_LOAD : (l + 1) * GROUPS_IN_LOAD, :, :])
-            for k in range(GROUPS_IN_LOAD):
-                flipped_group = flipped.tile([P, 2, P], BF16, name="flipped_group")
-                for j in range(2):
-                    nc.tensor.transpose(flipped_group[:, j, :], loaded[:, k, j, :], identity[:])
-                first = (l * GROUPS_IN_LOAD + k) * GROUP
-                columns = window[:, first : first + GROUP].rearrange("d (p j) -> d p j", j=2)
-                if k % 2 == 0:
-                    nc.vector.tensor_copy(columns, flipped_group[:].rearrange("d j p -> d p j"))
-                else:
-                    nc.scalar.copy(columns, flipped_group[:].rearrange("d j p -> d p j"))
+        table_groups = table.rearrange("(g j p) d -> g p j d", j=2, p=P)
+        for g in range(LOADS):
+            loaded = rows.tile([P, 2, P], BF16, name="loaded")
+            nc.sync.dma_start(loaded[:], table_groups[g])
+            flipped_group = flipped.tile([P, GROUP], BF16, name="flipped_group")
+            for j in range(2):
+                nc.tensor.transpose(flipped_group[:, j * P : (j + 1) * P], loaded[:, j, :], identity[:])
+            columns = window[:, g * GROUP : (g + 1) * GROUP]
+            if g % 2 == 0:
+                nc.vector.tensor_copy(columns, flipped_group[:])
+            else:
+                nc.scalar.copy(columns, flipped_group[:])
             nc.tensor.matmul(
-                nothing[:, :IDLE_COLUMNS],
-                identity[:],
-                loaded[:].rearrange("p k j d -> p (k j d)")[:, :IDLE_COLUMNS],
-                start=True,
-                stop=True,
+                nothing[:, :GROUP], identity[:], loaded[:].rearrange("p j d -> p (j d)"), start=True, stop=True
             )
 
         offsets = held.tile([P, PICKED // 16], U16, name="offsets")

@@ -55,7 +55,7 @@ def tile_testmmrsmodel_kernel(tc, table, w, offs, out):
         offsets = held.tile([P, PICKED // 16], U16, name="offsets")
         nc.sync.dma_start(offsets[:], offs)
         weights = held.tile([P, FEATURES_OUT], BF16, name="weights")
-        nc.gpsimd.dma_start(weights[:], w)
+        nc.sync.dma_start(weights[:], w)
 
         for h in range(FEATURES_OUT // P):
             product = products.tile([P, PICKED], F32, name="product")

@@ -9,7 +9,8 @@ FEATURES_OUT = 256
 PICKED = 512
 CHUNKS = 8
 CHUNK = PICKED // CHUNKS
-GROUP = 2 * P
+BLOCKS = 4
+GROUP = BLOCKS * P
 LOADS = STORE // GROUP
 WARM_UP = 4
 
@@ -36,18 +37,19 @@ def tile_testmmrsmodel_kernel(tc, table, w, offs, out):
         make_identity(nc, identity[:])
 
         window = held.tile([P, STORE], BF16, name="window")
-        table_groups = table.rearrange("(g j p) d -> g p j d", j=2, p=P)
+        table_groups = table.rearrange("(g p j) d -> g p j d", j=BLOCKS, p=P)
         for g in range(LOADS):
-            loaded = rows.tile([P, 2, P], BF16, name="loaded")
+            loaded = rows.tile([P, BLOCKS, P], BF16, name="loaded")
             nc.sync.dma_start(loaded[:], table_groups[g])
             flipped_group = flipped.tile([P, GROUP], BF16, name="flipped_group")
-            for j in range(2):
+            for j in range(BLOCKS):
                 nc.tensor.transpose(flipped_group[:, j * P : (j + 1) * P], loaded[:, j, :], identity[:])
-            columns = window[:, g * GROUP : (g + 1) * GROUP]
+            columns = window[:, g * GROUP : (g + 1) * GROUP].rearrange("d (p j) -> d p j", j=BLOCKS)
+            in_token_order = flipped_group[:].rearrange("d (j p) -> d p j", j=BLOCKS)
             if g % 2 == 0:
-                nc.vector.tensor_copy(columns, flipped_group[:])
+                nc.vector.tensor_copy(columns, in_token_order)
             else:
-                nc.scalar.copy(columns, flipped_group[:])
+                nc.scalar.copy(columns, in_token_order)
             nc.tensor.matmul(
                 nothing[:, :GROUP], identity[:], loaded[:].rearrange("p j d -> p (j d)"), start=True, stop=True
             )

@@ -9,10 +9,10 @@ FEATURES_OUT = 256
 PICKED = 512
 CHUNKS = 8
 CHUNK = PICKED // CHUNKS
-BLOCKS = 4
-GROUP = BLOCKS * P
-LOADS = STORE // GROUP
-WARM_UP = 4
+LOADS = (1024, 1024, 1024, 512, 256, 256)
+assert sum(LOADS) == STORE
+BANKS = 5
+WARM_UP = 16
 
 FLOPS = 2 * P * FEATURES_OUT * PICKED
 
@@ -21,38 +21,42 @@ def tile_testmmrsmodel_kernel(tc, table, w, offs, out):
     nc = tc.nc
     with (
         tc.tile_pool(name="held", bufs=1) as held,
-        tc.tile_pool(name="rows", bufs=LOADS) as rows,
+        tc.tile_pool(name="rows", bufs=1) as rows,
         tc.tile_pool(name="sums", bufs=2) as sums,
-        tc.psum_pool(name="flipped", bufs=5) as flipped,
+        tc.psum_pool(name="flipped", bufs=BANKS) as flipped,
         tc.psum_pool(name="products", bufs=2) as products,
         tc.psum_pool(name="unused", bufs=1) as unused,
     ):
-        zeros = held.tile([P, PICKED], BF16, name="zeros")
-        nc.vector.memset(zeros[:], 0.0)
         nothing = unused.tile([P, PICKED], F32, name="nothing")
+        zeros = held.tile([P, P], BF16, name="zeros")
+        nc.vector.memset(zeros[:], 0.0)
         for turn in range(WARM_UP):
-            nc.tensor.matmul(nothing[:], zeros[:, :P], zeros[:], start=True, stop=True)
+            nc.tensor.matmul(nothing[:, :P], zeros[:], zeros[:], start=True, stop=True)
 
         identity = held.tile([P, P], BF16, name="identity")
         make_identity(nc, identity[:])
 
         window = held.tile([P, STORE], BF16, name="window")
-        table_groups = table.rearrange("(g p j) d -> g p j d", j=BLOCKS, p=P)
-        for g in range(LOADS):
-            loaded = rows.tile([P, BLOCKS, P], BF16, name="loaded")
-            nc.sync.dma_start(loaded[:], table_groups[g])
-            flipped_group = flipped.tile([P, GROUP], BF16, name="flipped_group")
-            for j in range(BLOCKS):
+        first = 0
+        for g, group in enumerate(LOADS):
+            blocks = group // P
+            loaded = rows.tile([P, blocks, P], BF16, name="loaded%d" % g)
+            nc.sync.dma_start(loaded[:], table[first : first + group, :].rearrange("(p j) d -> p j d", j=blocks))
+            flipped_bank = flipped.tile([P, LOADS[0]], BF16, name="flipped_bank")
+            flipped_group = flipped_bank[:, :group]
+            for j in range(blocks):
                 nc.tensor.transpose(flipped_group[:, j * P : (j + 1) * P], loaded[:, j, :], identity[:])
-            columns = window[:, g * GROUP : (g + 1) * GROUP].rearrange("d (p j) -> d p j", j=BLOCKS)
-            in_token_order = flipped_group[:].rearrange("d (j p) -> d p j", j=BLOCKS)
+            columns = window[:, first : first + group].rearrange("d (p j) -> d p j", j=blocks)
+            in_token_order = flipped_group.rearrange("d (j p) -> d p j", j=blocks)
             if g % 2 == 0:
                 nc.vector.tensor_copy(columns, in_token_order)
             else:
                 nc.scalar.copy(columns, in_token_order)
-            nc.tensor.matmul(
-                nothing[:, :GROUP], identity[:], loaded[:].rearrange("p j d -> p (j d)"), start=True, stop=True
-            )
+            if group >= PICKED:
+                nc.tensor.matmul(
+                    nothing[:], identity[:], loaded[:].rearrange("p j d -> p (j d)")[:, :PICKED], start=True, stop=True
+                )
+            first += group
 
         offsets = held.tile([P, PICKED // 16], U16, name="offsets")
         nc.sync.dma_start(offsets[:], offs)
@@ -71,5 +75,4 @@ def tile_testmmrsmodel_kernel(tc, table, w, offs, out):
                 axis=mybir.AxisListType.X,
                 op=mybir.AluOpType.add,
             )
-            queue = nc.sync if h == 0 else nc.scalar
-            queue.dma_start(out[h * P : (h + 1) * P, :], summed[:])
+            nc.sync.dma_start(out[h * P : (h + 1) * P, :], summed[:])

import concourse.mybir as mybir
from concourse.masks import make_identity

BF16, F32, U16 = mybir.dt.bfloat16, mybir.dt.float32, mybir.dt.uint16

P = 128
STORE = 4096
FEATURES_OUT = 256
PICKED = 512
CHUNKS = 8
CHUNK = PICKED // CHUNKS
LOADS = (1024, 1024, 1024, 512, 256, 256)
assert sum(LOADS) == STORE
BANKS = 5
WARM_UP = 16

FLOPS = 2 * P * FEATURES_OUT * PICKED


def tile_testmmrsmodel_kernel(tc, table, w, offs, out):
    nc = tc.nc
    with (
        tc.tile_pool(name="held", bufs=1) as held,
        tc.tile_pool(name="rows", bufs=1) as rows,
        tc.tile_pool(name="sums", bufs=2) as sums,
        tc.psum_pool(name="flipped", bufs=BANKS) as flipped,
        tc.psum_pool(name="products", bufs=2) as products,
        tc.psum_pool(name="unused", bufs=1) as unused,
    ):
        nothing = unused.tile([P, PICKED], F32, name="nothing")
        zeros = held.tile([P, P], BF16, name="zeros")
        nc.vector.memset(zeros[:], 0.0)
        for turn in range(WARM_UP):
            nc.tensor.matmul(nothing[:, :P], zeros[:], zeros[:], start=True, stop=True)

        identity = held.tile([P, P], BF16, name="identity")
        make_identity(nc, identity[:])

        window = held.tile([P, STORE], BF16, name="window")
        first = 0
        for g, group in enumerate(LOADS):
            blocks = group // P
            loaded = rows.tile([P, blocks, P], BF16, name="loaded%d" % g)
            nc.sync.dma_start(loaded[:], table[first : first + group, :].rearrange("(p j) d -> p j d", j=blocks))
            flipped_bank = flipped.tile([P, LOADS[0]], BF16, name="flipped_bank")
            flipped_group = flipped_bank[:, :group]
            for j in range(blocks):
                nc.tensor.transpose(flipped_group[:, j * P : (j + 1) * P], loaded[:, j, :], identity[:])
            columns = window[:, first : first + group].rearrange("d (p j) -> d p j", j=blocks)
            in_token_order = flipped_group.rearrange("d (j p) -> d p j", j=blocks)
            if g % 2 == 0:
                nc.vector.tensor_copy(columns, in_token_order)
            else:
                nc.scalar.copy(columns, in_token_order)
            if group >= PICKED:
                nc.tensor.matmul(
                    nothing[:], identity[:], loaded[:].rearrange("p j d -> p (j d)")[:, :PICKED], start=True, stop=True
                )
            first += group

        offsets = held.tile([P, PICKED // 16], U16, name="offsets")
        nc.sync.dma_start(offsets[:], offs)
        weights = held.tile([P, FEATURES_OUT], BF16, name="weights")
        nc.sync.dma_start(weights[:], w)

        for h in range(FEATURES_OUT // P):
            product = products.tile([P, PICKED], F32, name="product")
            nc.tensor.matmul(
                product[:], weights[:, h * P : (h + 1) * P], window[:].indirect(offsets[:]), start=True, stop=True
            )
            summed = sums.tile([P, CHUNK], F32, name="summed")
            nc.vector.tensor_reduce(
                summed[:],
                product[:].rearrange("p (c r) -> p r c", c=CHUNKS),
                axis=mybir.AxisListType.X,
                op=mybir.AluOpType.add,
            )
            nc.sync.dma_start(out[h * P : (h + 1) * P, :], summed[:])
